import numpy as np
import ml_dtypes


def mxq(x, axis, fmt="e4m3"):
    dtype, down = {"e4m3": (ml_dtypes.float8_e4m3fn, 7), "e5m2": (ml_dtypes.float8_e5m2, 14)}[fmt]
    v = np.moveaxis(np.asarray(x, np.float32).astype(ml_dtypes.bfloat16).astype(np.float64), axis, -1)
    blocks = v.reshape(v.shape[:-1] + (-1, 32))
    amax = np.abs(blocks).max(-1, keepdims=True)
    byte = np.maximum(np.where(amax > 0, np.frexp(amax)[1] - 1 + 127, 0) - down, 1)
    scale = np.exp2(byte - 127.0)
    codes = (blocks / scale).astype(np.float32).astype(dtype).astype(np.float64)
    return np.moveaxis((codes * scale).reshape(v.shape), -1, axis)


WIDE = False


def mx_kscale(k):
    if not WIDE:
        return np.ones(k)
    levels = np.array([10, -10, 5, -5, 0])
    a = np.random.permutation(np.resize(levels, k // 512 * 4)).reshape(k // 512, 4)
    idx = np.arange(k)
    return np.exp2(a[idx // 512, idx % 128 // 32])


BF16 = ml_dtypes.bfloat16


def bf(x):
    return np.asarray(x, np.float32).astype(BF16)


def f64(x):
    return np.asarray(x).astype(np.float64)


E2M1 = np.array([0.0, 0.5, 1.0, 1.5, 2.0, 3.0, 4.0, 6.0, -0.0, -0.5, -1.0, -1.5, -2.0, -3.0, -4.0, -6.0])


def pack_weight(w, fmt):
    k, n = w.shape
    w = f64(bf(w)).reshape(k // 32, 32, n)
    amax = np.abs(w).max(1)
    if fmt == "e4m3":
        byte = np.frexp(amax)[1] - 1 + 127 - 7
    else:
        mant, ex = np.frexp(amax / 6.0)
        byte = np.where(mant > 0.5, ex, ex - 1) + 127
    byte = np.clip(np.where(amax > 0, byte, 1), 1, 254)
    scaled = (w * np.exp2(127.0 - byte)[:, None, :]).reshape(k, n).astype(np.float32)
    by_word = np.ascontiguousarray(scaled.reshape(k // 512, 128, 4, n).transpose(0, 1, 3, 2))
    if fmt == "e4m3":
        words = by_word.astype(ml_dtypes.float8_e4m3fn).view(np.uint8)
    else:
        c = by_word.astype(ml_dtypes.float4_e2m1fn).view(np.uint8) & 0xF
        words = c[..., 0::2] | (c[..., 1::2] << 4)
    return np.ascontiguousarray(words), np.ascontiguousarray(byte.astype(np.uint8).reshape(k // 512, 16, n))


def unpack_weight(words, scales, fmt):
    g, p, n, _ = words.shape
    if fmt == "e4m3":
        vals = np.ascontiguousarray(words).view(ml_dtypes.float8_e4m3fn).astype(np.float64)
    else:
        nib = np.empty((g, p, n, 4), np.uint8)
        nib[..., 0::2] = words & 0xF
        nib[..., 1::2] = words >> 4
        vals = E2M1[nib]
    vals = vals * np.repeat(np.exp2(scales.astype(np.float64) - 127.0), 8, axis=1)[..., None]
    return vals.transpose(0, 1, 3, 2).reshape(g * 512, n)


B, D, H = 1024, 1024, 1024


def setup_inputs():
    s = mx_kscale(D)
    h_c1 = bf(np.random.standard_normal((B, H)))
    h_c2 = bf(np.random.standard_normal((B, H)))
    x_t = bf(np.random.standard_normal((B, D)) * s)
    r_param = bf(np.random.uniform(0.1, 1.05, (1, H)))
    theta_param = bf(np.random.uniform(0.0, 2.0 * np.pi, (1, H)))
    w1_words, w1_scales = pack_weight(np.random.standard_normal((D, H)) / np.sqrt(D) / s[:, None], "e4m3")
    w2_words, w2_scales = pack_weight(np.random.standard_normal((D, H)) / np.sqrt(D) / s[:, None], "e4m3")
    return {"h_c1": h_c1,
            "h_c2": h_c2,
            "x_t": x_t,
            "r_param": r_param,
            "theta_param": theta_param,
            "w1_words": w1_words,
            "w1_scales": w1_scales,
            "w2_words": w2_words,
            "w2_scales": w2_scales}


def reference(h_c1, h_c2, x_t, r_param, theta_param, w1_words, w1_scales, w2_words, w2_scales):
    h_c1, h_c2 = f64(h_c1), f64(h_c2)
    r, theta = f64(r_param), f64(theta_param)
    g = r * np.cos(theta)
    phi = r * np.sin(theta)
    norm = np.sqrt(np.maximum(1.0 - r * r, 0.0))
    xq = mxq(f64(x_t), 1, "e4m3")
    w_c1_x = xq @ unpack_weight(w1_words, w1_scales, "e4m3")
    w_c2_x = xq @ unpack_weight(w2_words, w2_scales, "e4m3")
    h_t_c1 = g * h_c1 - phi * h_c2 + norm * w_c1_x
    h_t_c2 = g * h_c2 + phi * h_c1 + norm * w_c2_x
    h_t = np.maximum(np.concatenate((h_t_c1, h_t_c2), axis=-1), 0.0)
    return (h_t_c1, h_t_c2, h_t)

@@ -1,0 +1,288 @@
+from contextlib import ExitStack
+
+import concourse.mybir as mybir
+from concourse.masks import make_identity
+
+FP8X4 = mybir.dt.float8_e4m3fn_x4
+BF16 = mybir.dt.bfloat16
+F32 = mybir.dt.float32
+I32 = mybir.dt.int32
+U32 = mybir.dt.uint32
+U8 = mybir.dt.uint8
+ALU = mybir.AluOpType
+ACT = mybir.ActivationFunctionType
+
+B, D, H = 1024, 1024, 1024
+FLOPS = 2 * B * D * 2 * H
+
+P = 128
+PACK = 4
+K_PASS = P * PACK
+PASSES = D // K_PASS
+SUB = 2
+CHUNK = SUB * P
+CHUNKS = B // CHUNK
+N_TILES = H // P
+SIDES = 2
+ROUND_TILES = 2
+ROUNDS_PER_CHUNK = N_TILES // ROUND_TILES
+ROUNDS = CHUNKS * ROUNDS_PER_CHUNK
+STORE_TILES = 4
+LOAD_COLS = H // 2
+TINY = 1e-30
+FLOAT32_MAX = 3.4028234663852886e38
+
+
+def tile_linearrtus_kernel(
+    tc, h_c1, h_c2, x_t, r_param, theta_param, w1_words, w1_scales, w2_words, w2_scales, out_0, out_1, out_2
+):
+    nc = tc.nc
+    with ExitStack() as ctx:
+        keep = ctx.enter_context(tc.tile_pool(name="keep", bufs=1))
+        work = ctx.enter_context(tc.tile_pool(name="work", bufs=4))
+        outs = ctx.enter_context(tc.tile_pool(name="outs", bufs=3))
+        psum_acc = ctx.enter_context(tc.psum_pool(name="psum_acc", bufs=3))
+        psum_ht = ctx.enter_context(tc.psum_pool(name="psum_ht", bufs=2))
+        psum_back = ctx.enter_context(tc.psum_pool(name="psum_back", bufs=2))
+        psum_x = ctx.enter_context(tc.psum_pool(name="psum_x", bufs=1))
+        ctx.enter_context(tc.manual_schedule())
+
+        by_chunk = "(p c s) n -> p c s n"
+        x_rows = x_t.rearrange(by_chunk, c=CHUNKS, s=SUB)
+        h_rows = [h.rearrange(by_chunk, c=CHUNKS, s=SUB) for h in (h_c1, h_c2)]
+        state_rows = [o.rearrange(by_chunk, c=CHUNKS, s=SUB) for o in (out_0, out_1)]
+        relu_rows = out_2.rearrange("(p c s) (w n) -> p c s w n", c=CHUNKS, s=SUB, w=SIDES)
+        words_dram = (w1_words, w2_words)
+        scales_dram = (w1_scales, w2_scales)
+
+        x_sb = keep.tile([P, CHUNKS, SUB, D], BF16)
+        h1_sb = keep.tile([P, CHUNKS, SUB, H], BF16)
+        h2_sb = keep.tile([P, CHUNKS, SUB, H], BF16)
+        h_sb = (h1_sb, h2_sb)
+        w1_codes = keep.tile([P, PASSES, H], U32, align_bytes=64)
+        w2_codes = keep.tile([P, PASSES, H], U32, align_bytes=64)
+        w_codes = (w1_codes, w2_codes)
+        w_planes = keep.tile([P, H], U8, align_bytes=64)
+        x_grouped = keep.tile([P, CHUNKS, PASSES * CHUNK * PACK], BF16, align_bytes=64)
+        x_codes = keep.tile([P, CHUNKS, PASSES * CHUNK], U32, align_bytes=64)
+        x_planes = keep.tile([P, CHUNKS, PASSES * CHUNK], U8, align_bytes=64)
+        param_rows = keep.tile([P, P], BF16)
+        ident_bf16 = keep.tile([P, P], BF16)
+        ident_f32 = keep.tile([P, P], F32)
+
+        nc.vector.memset(w_planes[:].bitcast(I32), 0)
+        nc.vector.memset(param_rows[:], 0.0)
+        make_identity(nc, ident_bf16[:])
+        make_identity(nc, ident_f32[:])
+
+        def load_weight_half(half):
+            cols = slice(half * LOAD_COLS, (half + 1) * LOAD_COLS)
+            byte_cols = slice(half * LOAD_COLS * PACK, (half + 1) * LOAD_COLS * PACK)
+            for w in range(SIDES):
+                for g in range(PASSES):
+                    nc.sync.dma_start(
+                        out=w_codes[w][:, g, cols].bitcast(I32),
+                        in_=words_dram[w][g].rearrange("p n t -> p (n t)")[:, byte_cols].bitcast(I32),
+                    )
+
+        def load_h(c):
+            for side in range(SIDES):
+                nc.sync.dma_start(out=h_sb[side][:, c], in_=h_rows[side][:, c])
+
+        nc.sync.dma_start(out=param_rows[0:N_TILES, :], in_=r_param.rearrange("o (j n) -> (o j) n", n=P))
+        nc.sync.dma_start(
+            out=param_rows[N_TILES : 2 * N_TILES, :], in_=theta_param.rearrange("o (j n) -> (o j) n", n=P)
+        )
+        nc.sync.dma_start(out=x_sb[:, 0], in_=x_rows[:, 0])
+        for w in range(SIDES):
+            for quadrant in range(4):
+                first = 32 * quadrant + 8 * w
+                nc.sync.dma_start(
+                    out=w_planes[first : first + 8, :].bitcast(I32),
+                    in_=scales_dram[w][:, 4 * quadrant : 4 * quadrant + 4, :].bitcast(I32),
+                )
+        load_weight_half(0)
+        load_h(0)
+        load_weight_half(1)
+        for c in range(1, CHUNKS):
+            nc.sync.dma_start(out=x_sb[:, c], in_=x_rows[:, c])
+            load_h(c)
+
+        param_ps = psum_x.tile([P, P], BF16, tag="xt")
+        nc.tensor.transpose(param_ps[:], param_rows[:], ident_bf16[:])
+        params = keep.tile([P, 2 * N_TILES], F32)
+        nc.vector.tensor_copy(out=params[:], in_=param_ps[:, 0 : 2 * N_TILES])
+        radius = params[:, 0:N_TILES]
+        theta = params[:, N_TILES : 2 * N_TILES]
+
+        sin_half = keep.tile([P, N_TILES], F32)
+        sin_quarter = keep.tile([P, N_TILES], F32)
+        cos_half = keep.tile([P, N_TILES], F32)
+        cos_full = keep.tile([P, N_TILES], F32)
+        gain = keep.tile([P, N_TILES], F32)
+        phi = keep.tile([P, N_TILES], F32)
+        neg_phi = keep.tile([P, N_TILES], F32)
+        room = keep.tile([P, N_TILES], F32)
+        is_open = keep.tile([P, N_TILES], F32)
+        root = keep.tile([P, N_TILES], F32)
+        norm = keep.tile([P, N_TILES], F32)
+        nc.scalar.activation(out=sin_half[:], in_=theta, func=ACT.Sin, scale=0.5)
+        nc.scalar.activation(out=sin_quarter[:], in_=theta, func=ACT.Sin, scale=0.25)
+        nc.vector.tensor_tensor(out=room[:], in0=radius, in1=radius, op=ALU.mult)
+        nc.vector.tensor_scalar(out=room[:], in0=room[:], scalar1=-1.0, scalar2=1.0, op0=ALU.mult, op1=ALU.add)
+        nc.vector.tensor_single_scalar(out=is_open[:], in_=room[:], scalar=0.0, op=ALU.is_gt)
+        nc.vector.tensor_scalar_max(out=room[:], in0=room[:], scalar1=TINY)
+        nc.scalar.activation(out=root[:], in_=room[:], func=ACT.Sqrt)
+
+        def finish_params():
+            nc.vector.tensor_tensor(out=cos_full[:], in0=sin_half[:], in1=sin_half[:], op=ALU.mult)
+            nc.vector.tensor_scalar(
+                out=cos_full[:], in0=cos_full[:], scalar1=-2.0, scalar2=1.0, op0=ALU.mult, op1=ALU.add
+            )
+            nc.vector.tensor_tensor(out=gain[:], in0=cos_full[:], in1=radius, op=ALU.mult)
+            nc.vector.tensor_tensor(out=cos_half[:], in0=sin_quarter[:], in1=sin_quarter[:], op=ALU.mult)
+            nc.vector.tensor_scalar(
+                out=cos_half[:], in0=cos_half[:], scalar1=-2.0, scalar2=1.0, op0=ALU.mult, op1=ALU.add
+            )
+            nc.vector.tensor_tensor(out=phi[:], in0=sin_half[:], in1=cos_half[:], op=ALU.mult)
+            nc.vector.scalar_tensor_tensor(
+                out=phi[:], in0=phi[:], scalar=2.0, in1=radius, op0=ALU.mult, op1=ALU.mult
+            )
+            nc.vector.tensor_scalar_mul(out=neg_phi[:], in0=phi[:], scalar1=-1.0)
+            nc.vector.tensor_tensor(out=norm[:], in0=root[:], in1=is_open[:], op=ALU.mult)
+
+        def transpose_x(c, g):
+            xt = psum_x.tile([P, 2, CHUNK], F32, tag="xt")
+            for u in range(2):
+                for s in range(SUB):
+                    words = x_sb[:, c, s, :].bitcast(F32)
+                    first = g * (K_PASS // 2) + u
+                    nc.tensor.transpose(
+                        xt[:, u, s * P : (s + 1) * P], words[:, first : (g + 1) * (K_PASS // 2) : 2], ident_f32[:]
+                    )
+            pairs = x_grouped[:, c, :].bitcast(F32).rearrange("q (g b u) -> q g b u", g=PASSES, u=2)
+            nc.vector.tensor_copy(out=pairs[:, g], in_=xt[:].rearrange("q u b -> q b u"))
+
+        def quantise_x(c):
+            nc.vector.quantize_mx(
+                out=x_codes[:, c, :].bitcast(FP8X4), scales=x_planes[:, c, :], in_=x_grouped[:, c, :]
+            )
+
+        ht_of = {}
+        acc_of = {}
+        state_of = {}
+        out_of = {}
+
+        def place(i):
+            return i // ROUNDS_PER_CHUNK, (i % ROUNDS_PER_CHUNK) * ROUND_TILES
+
+        def transpose_h(i):
+            c, first_tile = place(i)
+            ht = psum_ht.tile([P, ROUND_TILES, SIDES, CHUNK], BF16)
+            for t in range(ROUND_TILES):
+                n_cols = slice((first_tile + t) * P, (first_tile + t + 1) * P)
+                for side in range(SIDES):
+                    for s in range(SUB):
+                        nc.tensor.transpose(
+                            ht[:, t, side, s * P : (s + 1) * P], h_sb[side][:, c, s, n_cols], ident_bf16[:]
+                        )
+            ht_of[i] = ht
+
+        def multiply(i):
+            c, first_tile = place(i)
+            for t in range(ROUND_TILES):
+                n_cols = slice((first_tile + t) * P, (first_tile + t + 1) * P)
+                acc = psum_acc.tile([P, SIDES, CHUNK], F32)
+                for w in range(SIDES):
+                    for g in range(PASSES):
+                        b_cols = slice(g * CHUNK, (g + 1) * CHUNK)
+                        nc.tensor.matmul_mx(
+                            out=acc[:, w, :],
+                            lhsT=w_codes[w][:, g, n_cols].bitcast(FP8X4),
+                            lhsT_scale=w_planes[8 * w + 4 * g : P, n_cols],
+                            rhs=x_codes[:, c, b_cols].bitcast(FP8X4),
+                            rhs_scale=x_planes[:, c, b_cols],
+                            start=(g == 0),
+                            stop=(g == PASSES - 1),
+                        )
+                acc_of[(i, t)] = acc
+
+        def combine(i):
+            first_tile = place(i)[1]
+            ht = ht_of[i]
+            partial_of = {}
+            for t in range(ROUND_TILES):
+                j = first_tile + t
+                scaled = work.tile([P, SIDES, CHUNK], F32)
+                nc.scalar.activation(
+                    out=scaled[:], in_=acc_of[(i, t)][:], func=ACT.Copy, scale=norm[:, j : j + 1]
+                )
+                partial = work.tile([P, SIDES, CHUNK], F32)
+                nc.vector.scalar_tensor_tensor(
+                    out=partial[:], in0=ht[:, t], scalar=gain[:, j : j + 1], in1=scaled[:], op0=ALU.mult, op1=ALU.add
+                )
+                partial_of[t] = partial
+            for t in range(ROUND_TILES):
+                j = first_tile + t
+                state = work.tile([P, SIDES, CHUNK], F32)
+                nc.vector.scalar_tensor_tensor(
+                    out=state[:, 0], in0=ht[:, t, 1], scalar=neg_phi[:, j : j + 1], in1=partial_of[t][:, 0],
+                    op0=ALU.mult, op1=ALU.add,
+                )
+                nc.vector.scalar_tensor_tensor(
+                    out=state[:, 1], in0=ht[:, t, 0], scalar=phi[:, j : j + 1], in1=partial_of[t][:, 1],
+                    op0=ALU.mult, op1=ALU.add,
+                )
+                state_of[(i, t)] = state
+
+        def finish(i):
+            c, first_tile = place(i)
+            group_tile = first_tile % STORE_TILES
+            if group_tile == 0:
+                plain = outs.tile([P, SIDES, SUB, STORE_TILES * P], F32)
+                relu = outs.tile([P, SIDES, SUB, STORE_TILES * P], F32)
+                out_of["plain"] = plain
+                out_of["relu"] = relu
+            plain = out_of["plain"]
+            relu = out_of["relu"]
+            for t in range(ROUND_TILES):
+                state = state_of[(i, t)]
+                back = psum_back.tile([P, SIDES, SUB, P], F32)
+                for w in range(SIDES):
+                    for s in range(SUB):
+                        nc.tensor.transpose(back[:, w, s, :], state[:, w, s * P : (s + 1) * P], ident_f32[:])
+                cols = slice((group_tile + t) * P, (group_tile + t + 1) * P)
+                nc.scalar.copy(out=plain[:, :, :, cols], in_=back[:])
+            cols = slice(group_tile * P, (group_tile + ROUND_TILES) * P)
+            nc.gpsimd.tensor_scalar(
+                out=relu[:, :, :, cols], in0=plain[:, :, :, cols], scalar1=FLOAT32_MAX, scalar2=0.0,
+                op0=ALU.min, op1=ALU.max,
+            )
+            if group_tile + ROUND_TILES == STORE_TILES:
+                n_cols = slice((first_tile + ROUND_TILES - STORE_TILES) * P, (first_tile + ROUND_TILES) * P)
+                for w in range(SIDES):
+                    nc.sync.dma_start(out=state_rows[w][:, c, :, n_cols], in_=plain[:, w])
+                    nc.sync.dma_start(out=relu_rows[:, c, :, w, n_cols], in_=relu[:, w])
+
+        for g in range(PASSES):
+            transpose_x(0, g)
+        quantise_x(0)
+        finish_params()
+        multiply(0)
+        transpose_h(0)
+        transpose_h(1)
+        for i in range(ROUNDS + 1):
+            next_chunk = i // ROUNDS_PER_CHUNK + 1
+            step = i % ROUNDS_PER_CHUNK
+            if next_chunk < CHUNKS and step == PASSES + 1:
+                quantise_x(next_chunk)
+            if i < ROUNDS:
+                combine(i)
+            if i + 1 < ROUNDS:
+                multiply(i + 1)
+            if i >= 1:
+                finish(i - 1)
+            if next_chunk < CHUNKS and 1 <= step <= PASSES:
+                transpose_x(next_chunk, step - 1)
+            if i + 2 < ROUNDS:
+                transpose_h(i + 2)

@@ -30,7 +30,6 @@ ROUNDS = CHUNKS * ROUNDS_PER_CHUNK
 STORE_TILES = 4
 LOAD_COLS = H // 2
 TINY = 1e-30
-FLOAT32_MAX = 3.4028234663852886e38
 
 
 def tile_linearrtus_kernel(
@@ -161,7 +160,7 @@ def tile_linearrtus_kernel(
                         xt[:, u, s * P : (s + 1) * P], words[:, first : (g + 1) * (K_PASS // 2) : 2], ident_f32[:]
                     )
             pairs = x_grouped[:, c, :].bitcast(F32).rearrange("q (g b u) -> q g b u", g=PASSES, u=2)
-            nc.vector.tensor_copy(out=pairs[:, g], in_=xt[:].rearrange("q u b -> q b u"))
+            nc.scalar.copy(out=pairs[:, g], in_=xt[:].rearrange("q u b -> q b u"))
 
         def quantise_x(c):
             nc.vector.quantize_mx(
@@ -254,10 +253,7 @@ def tile_linearrtus_kernel(
                 cols = slice((group_tile + t) * P, (group_tile + t + 1) * P)
                 nc.scalar.copy(out=plain[:, :, :, cols], in_=back[:])
             cols = slice(group_tile * P, (group_tile + ROUND_TILES) * P)
-            nc.gpsimd.tensor_scalar(
-                out=relu[:, :, :, cols], in0=plain[:, :, :, cols], scalar1=FLOAT32_MAX, scalar2=0.0,
-                op0=ALU.min, op1=ALU.max,
-            )
+            nc.vector.tensor_scalar_max(out=relu[:, :, :, cols], in0=plain[:, :, :, cols], scalar1=0.0)
             if group_tile + ROUND_TILES == STORE_TILES:
                 n_cols = slice((first_tile + ROUND_TILES - STORE_TILES) * P, (first_tile + ROUND_TILES) * P)
                 for w in range(SIDES):

@@ -28,8 +28,10 @@ ROUND_TILES = 2
 ROUNDS_PER_CHUNK = N_TILES // ROUND_TILES
 ROUNDS = CHUNKS * ROUNDS_PER_CHUNK
 STORE_TILES = 4
+STORE_ROUNDS = STORE_TILES // ROUND_TILES
 LOAD_COLS = H // 2
 TINY = 1e-30
+FLOAT32_MAX = 3.4028234663852886e38
 
 
 def tile_linearrtus_kernel(
@@ -38,12 +40,11 @@ def tile_linearrtus_kernel(
     nc = tc.nc
     with ExitStack() as ctx:
         keep = ctx.enter_context(tc.tile_pool(name="keep", bufs=1))
-        work = ctx.enter_context(tc.tile_pool(name="work", bufs=4))
+        work = ctx.enter_context(tc.tile_pool(name="work", bufs=3 * ROUND_TILES))
         outs = ctx.enter_context(tc.tile_pool(name="outs", bufs=3))
         psum_acc = ctx.enter_context(tc.psum_pool(name="psum_acc", bufs=3))
         psum_ht = ctx.enter_context(tc.psum_pool(name="psum_ht", bufs=2))
-        psum_back = ctx.enter_context(tc.psum_pool(name="psum_back", bufs=2))
-        psum_x = ctx.enter_context(tc.psum_pool(name="psum_x", bufs=1))
+        psum_back = ctx.enter_context(tc.psum_pool(name="psum_back", bufs=3))
         ctx.enter_context(tc.manual_schedule())
 
         by_chunk = "(p c s) n -> p c s n"
@@ -92,7 +93,8 @@ def tile_linearrtus_kernel(
         nc.sync.dma_start(
             out=param_rows[N_TILES : 2 * N_TILES, :], in_=theta_param.rearrange("o (j n) -> (o j) n", n=P)
         )
-        nc.sync.dma_start(out=x_sb[:, 0], in_=x_rows[:, 0])
+        for c in range(CHUNKS):
+            nc.sync.dma_start(out=x_sb[:, c], in_=x_rows[:, c])
         for w in range(SIDES):
             for quadrant in range(4):
                 first = 32 * quadrant + 8 * w
@@ -104,10 +106,9 @@ def tile_linearrtus_kernel(
         load_h(0)
         load_weight_half(1)
         for c in range(1, CHUNKS):
-            nc.sync.dma_start(out=x_sb[:, c], in_=x_rows[:, c])
             load_h(c)
 
-        param_ps = psum_x.tile([P, P], BF16, tag="xt")
+        param_ps = psum_back.tile([P, P], BF16, tag="back")
         nc.tensor.transpose(param_ps[:], param_rows[:], ident_bf16[:])
         params = keep.tile([P, 2 * N_TILES], F32)
         nc.vector.tensor_copy(out=params[:], in_=param_ps[:, 0 : 2 * N_TILES])
@@ -151,7 +152,7 @@ def tile_linearrtus_kernel(
             nc.vector.tensor_tensor(out=norm[:], in0=root[:], in1=is_open[:], op=ALU.mult)
 
         def transpose_x(c, g):
-            xt = psum_x.tile([P, 2, CHUNK], F32, tag="xt")
+            xt = psum_back.tile([P, 2, CHUNK], F32, tag="back")
             for u in range(2):
                 for s in range(SUB):
                     words = x_sb[:, c, s, :].bitcast(F32)
@@ -160,7 +161,10 @@ def tile_linearrtus_kernel(
                         xt[:, u, s * P : (s + 1) * P], words[:, first : (g + 1) * (K_PASS // 2) : 2], ident_f32[:]
                     )
             pairs = x_grouped[:, c, :].bitcast(F32).rearrange("q (g b u) -> q g b u", g=PASSES, u=2)
-            nc.scalar.copy(out=pairs[:, g], in_=xt[:].rearrange("q u b -> q b u"))
+            if g == 0:
+                nc.vector.tensor_copy(out=pairs[:, g], in_=xt[:].rearrange("q u b -> q b u"))
+            else:
+                nc.scalar.copy(out=pairs[:, g], in_=xt[:].rearrange("q u b -> q b u"))
 
         def quantise_x(c):
             nc.vector.quantize_mx(
@@ -169,6 +173,7 @@ def tile_linearrtus_kernel(
 
         ht_of = {}
         acc_of = {}
+        scaled_of = {}
         state_of = {}
         out_of = {}
 
@@ -206,19 +211,24 @@ def tile_linearrtus_kernel(
                         )
                 acc_of[(i, t)] = acc
 
-        def combine(i):
+        def scale(i):
+            first_tile = place(i)[1]
+            for t in range(ROUND_TILES):
+                j = first_tile + t
+                scaled = work.tile([P, SIDES, CHUNK], F32)
+                nc.scalar.activation(out=scaled[:], in_=acc_of[(i, t)][:], func=ACT.Copy, scale=norm[:, j : j + 1])
+                scaled_of[(i, t)] = scaled
+
+        def rotate(i):
             first_tile = place(i)[1]
             ht = ht_of[i]
             partial_of = {}
             for t in range(ROUND_TILES):
                 j = first_tile + t
-                scaled = work.tile([P, SIDES, CHUNK], F32)
-                nc.scalar.activation(
-                    out=scaled[:], in_=acc_of[(i, t)][:], func=ACT.Copy, scale=norm[:, j : j + 1]
-                )
                 partial = work.tile([P, SIDES, CHUNK], F32)
                 nc.vector.scalar_tensor_tensor(
-                    out=partial[:], in0=ht[:, t], scalar=gain[:, j : j + 1], in1=scaled[:], op0=ALU.mult, op1=ALU.add
+                    out=partial[:], in0=ht[:, t], scalar=gain[:, j : j + 1], in1=scaled_of[(i, t)][:],
+                    op0=ALU.mult, op1=ALU.add,
                 )
                 partial_of[t] = partial
             for t in range(ROUND_TILES):
@@ -234,16 +244,13 @@ def tile_linearrtus_kernel(
                 )
                 state_of[(i, t)] = state
 
-        def finish(i):
-            c, first_tile = place(i)
-            group_tile = first_tile % STORE_TILES
+        def transpose_back(i):
+            group_tile = place(i)[1] % STORE_TILES
             if group_tile == 0:
                 plain = outs.tile([P, SIDES, SUB, STORE_TILES * P], F32)
                 relu = outs.tile([P, SIDES, SUB, STORE_TILES * P], F32)
-                out_of["plain"] = plain
-                out_of["relu"] = relu
-            plain = out_of["plain"]
-            relu = out_of["relu"]
+                out_of[i // STORE_ROUNDS] = (plain, relu)
+            plain = out_of[i // STORE_ROUNDS][0]
             for t in range(ROUND_TILES):
                 state = state_of[(i, t)]
                 back = psum_back.tile([P, SIDES, SUB, P], F32)
@@ -252,33 +259,42 @@ def tile_linearrtus_kernel(
                         nc.tensor.transpose(back[:, w, s, :], state[:, w, s * P : (s + 1) * P], ident_f32[:])
                 cols = slice((group_tile + t) * P, (group_tile + t + 1) * P)
                 nc.scalar.copy(out=plain[:, :, :, cols], in_=back[:])
+
+        def relu_and_store(i):
+            c, first_tile = place(i)
+            group_tile = first_tile % STORE_TILES
+            plain, relu = out_of[i // STORE_ROUNDS]
             cols = slice(group_tile * P, (group_tile + ROUND_TILES) * P)
-            nc.vector.tensor_scalar_max(out=relu[:, :, :, cols], in0=plain[:, :, :, cols], scalar1=0.0)
+            nc.gpsimd.tensor_scalar(
+                out=relu[:, :, :, cols], in0=plain[:, :, :, cols], scalar1=FLOAT32_MAX, scalar2=0.0,
+                op0=ALU.min, op1=ALU.max,
+            )
             if group_tile + ROUND_TILES == STORE_TILES:
                 n_cols = slice((first_tile + ROUND_TILES - STORE_TILES) * P, (first_tile + ROUND_TILES) * P)
                 for w in range(SIDES):
                     nc.sync.dma_start(out=state_rows[w][:, c, :, n_cols], in_=plain[:, w])
+                for w in range(SIDES):
                     nc.sync.dma_start(out=relu_rows[:, c, :, w, n_cols], in_=relu[:, w])
 
-        for g in range(PASSES):
-            transpose_x(0, g)
-        quantise_x(0)
+        for c in range(CHUNKS):
+            for g in range(PASSES):
+                transpose_x(c, g)
+            if c >= 1:
+                quantise_x(c - 1)
+        quantise_x(CHUNKS - 1)
         finish_params()
         multiply(0)
+        scale(0)
         transpose_h(0)
-        transpose_h(1)
         for i in range(ROUNDS + 1):
-            next_chunk = i // ROUNDS_PER_CHUNK + 1
-            step = i % ROUNDS_PER_CHUNK
-            if next_chunk < CHUNKS and step == PASSES + 1:
-                quantise_x(next_chunk)
-            if i < ROUNDS:
-                combine(i)
             if i + 1 < ROUNDS:
                 multiply(i + 1)
+                scale(i + 1)
             if i >= 1:
-                finish(i - 1)
-            if next_chunk < CHUNKS and 1 <= step <= PASSES:
-                transpose_x(next_chunk, step - 1)
-            if i + 2 < ROUNDS:
-                transpose_h(i + 2)
+                transpose_back(i - 1)
+            if i + 1 < ROUNDS:
+                transpose_h(i + 1)
+            if i < ROUNDS:
+                rotate(i)
+            if i >= 1:
+                relu_and_store(i - 1)

@@ -29,7 +29,8 @@ ROUNDS_PER_CHUNK = N_TILES // ROUND_TILES
 ROUNDS = CHUNKS * ROUNDS_PER_CHUNK
 STORE_TILES = 4
 STORE_ROUNDS = STORE_TILES // ROUND_TILES
-LOAD_COLS = H // 2
+LOAD_COLS = ROUND_TILES * P
+FIRST_H_PIECES = 2
 TINY = 1e-30
 FLOAT32_MAX = 3.4028234663852886e38
 
@@ -41,7 +42,7 @@ def tile_linearrtus_kernel(
     with ExitStack() as ctx:
         keep = ctx.enter_context(tc.tile_pool(name="keep", bufs=1))
         work = ctx.enter_context(tc.tile_pool(name="work", bufs=3 * ROUND_TILES))
-        outs = ctx.enter_context(tc.tile_pool(name="outs", bufs=3))
+        outs = ctx.enter_context(tc.tile_pool(name="outs", bufs=4))
         psum_acc = ctx.enter_context(tc.psum_pool(name="psum_acc", bufs=3))
         psum_ht = ctx.enter_context(tc.psum_pool(name="psum_ht", bufs=2))
         psum_back = ctx.enter_context(tc.psum_pool(name="psum_back", bufs=3))
@@ -56,9 +57,14 @@ def tile_linearrtus_kernel(
         scales_dram = (w1_scales, w2_scales)
 
         x_sb = keep.tile([P, CHUNKS, SUB, D], BF16)
-        h1_sb = keep.tile([P, CHUNKS, SUB, H], BF16)
-        h2_sb = keep.tile([P, CHUNKS, SUB, H], BF16)
-        h_sb = (h1_sb, h2_sb)
+        h_sb = {}
+        for side in range(SIDES):
+            for c in range(CHUNKS):
+                pieces = FIRST_H_PIECES if c == 0 else 1
+                h_sb[(side, c)] = [
+                    keep.tile([P, SUB, H // pieces], BF16, name="h%d_%d_%d" % (side, c, piece))
+                    for piece in range(pieces)
+                ]
         w1_codes = keep.tile([P, PASSES, H], U32, align_bytes=64)
         w2_codes = keep.tile([P, PASSES, H], U32, align_bytes=64)
         w_codes = (w1_codes, w2_codes)
@@ -75,39 +81,56 @@ def tile_linearrtus_kernel(
         make_identity(nc, ident_bf16[:])
         make_identity(nc, ident_f32[:])
 
-        def load_weight_half(half):
-            cols = slice(half * LOAD_COLS, (half + 1) * LOAD_COLS)
-            byte_cols = slice(half * LOAD_COLS * PACK, (half + 1) * LOAD_COLS * PACK)
+        def load_weights(piece):
+            cols = slice(piece * LOAD_COLS, (piece + 1) * LOAD_COLS)
+            byte_cols = slice(piece * LOAD_COLS * PACK, (piece + 1) * LOAD_COLS * PACK)
             for w in range(SIDES):
-                for g in range(PASSES):
-                    nc.sync.dma_start(
-                        out=w_codes[w][:, g, cols].bitcast(I32),
-                        in_=words_dram[w][g].rearrange("p n t -> p (n t)")[:, byte_cols].bitcast(I32),
-                    )
+                nc.sync.dma_start(
+                    out=w_codes[w][:, :, cols].bitcast(I32),
+                    in_=words_dram[w].rearrange("g p n t -> p g (n t)")[:, :, byte_cols].bitcast(I32),
+                )
 
-        def load_h(c):
+        def load_h(c, piece):
             for side in range(SIDES):
-                nc.sync.dma_start(out=h_sb[side][:, c], in_=h_rows[side][:, c])
+                width = H // len(h_sb[(side, c)])
+                nc.sync.dma_start(
+                    out=h_sb[(side, c)][piece][:], in_=h_rows[side][:, c, :, piece * width : (piece + 1) * width]
+                )
+
+        def load_x(c):
+            nc.sync.dma_start(out=x_sb[:, c], in_=x_rows[:, c])
 
         nc.sync.dma_start(out=param_rows[0:N_TILES, :], in_=r_param.rearrange("o (j n) -> (o j) n", n=P))
         nc.sync.dma_start(
             out=param_rows[N_TILES : 2 * N_TILES, :], in_=theta_param.rearrange("o (j n) -> (o j) n", n=P)
         )
-        for c in range(CHUNKS):
-            nc.sync.dma_start(out=x_sb[:, c], in_=x_rows[:, c])
-        for w in range(SIDES):
+        def load_scales(w):
             for quadrant in range(4):
                 first = 32 * quadrant + 8 * w
                 nc.sync.dma_start(
                     out=w_planes[first : first + 8, :].bitcast(I32),
                     in_=scales_dram[w][:, 4 * quadrant : 4 * quadrant + 4, :].bitcast(I32),
                 )
-        load_weight_half(0)
-        load_h(0)
-        load_weight_half(1)
-        for c in range(1, CHUNKS):
-            load_h(c)
 
+        load_x(0)
+        load_x(1)
+        load_scales(0)
+        load_x(2)
+        load_x(3)
+        load_scales(1)
+        load_weights(0)
+        load_h(0, 0)
+        load_weights(1)
+        load_weights(2)
+        load_h(0, 1)
+        load_weights(3)
+        for c in range(1, CHUNKS):
+            load_h(c, 0)
+
+        one = keep.tile([P, 1], F32)
+        warm = keep.tile([P, 1], F32)
+        nc.vector.memset(one[:], 1.0)
+        nc.scalar.activation(out=warm[:], in_=one[:], func=ACT.Sqrt)
         param_ps = psum_back.tile([P, P], BF16, tag="back")
         nc.tensor.transpose(param_ps[:], param_rows[:], ident_bf16[:])
         params = keep.tile([P, 2 * N_TILES], F32)
@@ -126,15 +149,18 @@ def tile_linearrtus_kernel(
         is_open = keep.tile([P, N_TILES], F32)
         root = keep.tile([P, N_TILES], F32)
         norm = keep.tile([P, N_TILES], F32)
-        nc.scalar.activation(out=sin_half[:], in_=theta, func=ACT.Sin, scale=0.5)
-        nc.scalar.activation(out=sin_quarter[:], in_=theta, func=ACT.Sin, scale=0.25)
         nc.vector.tensor_tensor(out=room[:], in0=radius, in1=radius, op=ALU.mult)
         nc.vector.tensor_scalar(out=room[:], in0=room[:], scalar1=-1.0, scalar2=1.0, op0=ALU.mult, op1=ALU.add)
         nc.vector.tensor_single_scalar(out=is_open[:], in_=room[:], scalar=0.0, op=ALU.is_gt)
         nc.vector.tensor_scalar_max(out=room[:], in0=room[:], scalar1=TINY)
         nc.scalar.activation(out=root[:], in_=room[:], func=ACT.Sqrt)
+        nc.scalar.activation(out=sin_half[:], in_=theta, func=ACT.Sin, scale=0.5)
+        nc.scalar.activation(out=sin_quarter[:], in_=theta, func=ACT.Sin, scale=0.25)
 
-        def finish_params():
+        def finish_norm():
+            nc.vector.tensor_tensor(out=norm[:], in0=root[:], in1=is_open[:], op=ALU.mult)
+
+        def finish_rotation():
             nc.vector.tensor_tensor(out=cos_full[:], in0=sin_half[:], in1=sin_half[:], op=ALU.mult)
             nc.vector.tensor_scalar(
                 out=cos_full[:], in0=cos_full[:], scalar1=-2.0, scalar2=1.0, op0=ALU.mult, op1=ALU.add
@@ -149,7 +175,8 @@ def tile_linearrtus_kernel(
                 out=phi[:], in0=phi[:], scalar=2.0, in1=radius, op0=ALU.mult, op1=ALU.mult
             )
             nc.vector.tensor_scalar_mul(out=neg_phi[:], in0=phi[:], scalar1=-1.0)
-            nc.vector.tensor_tensor(out=norm[:], in0=root[:], in1=is_open[:], op=ALU.mult)
+
+        xt_of = {}
 
         def transpose_x(c, g):
             xt = psum_back.tile([P, 2, CHUNK], F32, tag="back")
@@ -160,6 +187,10 @@ def tile_linearrtus_kernel(
                     nc.tensor.transpose(
                         xt[:, u, s * P : (s + 1) * P], words[:, first : (g + 1) * (K_PASS // 2) : 2], ident_f32[:]
                     )
+            xt_of[(c, g)] = xt
+
+        def copy_x(c, g):
+            xt = xt_of[(c, g)]
             pairs = x_grouped[:, c, :].bitcast(F32).rearrange("q (g b u) -> q g b u", g=PASSES, u=2)
             if g == 0:
                 nc.vector.tensor_copy(out=pairs[:, g], in_=xt[:].rearrange("q u b -> q b u"))
@@ -180,15 +211,20 @@ def tile_linearrtus_kernel(
         def place(i):
             return i // ROUNDS_PER_CHUNK, (i % ROUNDS_PER_CHUNK) * ROUND_TILES
 
+        def h_block(side, c, s, j):
+            pieces = h_sb[(side, c)]
+            tiles_per_piece = N_TILES // len(pieces)
+            local = j % tiles_per_piece
+            return pieces[j // tiles_per_piece][:, s, local * P : (local + 1) * P]
+
         def transpose_h(i):
             c, first_tile = place(i)
             ht = psum_ht.tile([P, ROUND_TILES, SIDES, CHUNK], BF16)
             for t in range(ROUND_TILES):
-                n_cols = slice((first_tile + t) * P, (first_tile + t + 1) * P)
                 for side in range(SIDES):
                     for s in range(SUB):
                         nc.tensor.transpose(
-                            ht[:, t, side, s * P : (s + 1) * P], h_sb[side][:, c, s, n_cols], ident_bf16[:]
+                            ht[:, t, side, s * P : (s + 1) * P], h_block(side, c, s, first_tile + t), ident_bf16[:]
                         )
             ht_of[i] = ht
 
@@ -279,10 +315,12 @@ def tile_linearrtus_kernel(
         for c in range(CHUNKS):
             for g in range(PASSES):
                 transpose_x(c, g)
+                copy_x(c, g)
             if c >= 1:
                 quantise_x(c - 1)
         quantise_x(CHUNKS - 1)
-        finish_params()
+        finish_norm()
+        finish_rotation()
         multiply(0)
         scale(0)
         transpose_h(0)

@@ -31,6 +31,7 @@ STORE_TILES = 4
 STORE_ROUNDS = STORE_TILES // ROUND_TILES
 LOAD_COLS = ROUND_TILES * P
 FIRST_H_PIECES = 2
+WARM_FIRST = 5
 TINY = 1e-30
 FLOAT32_MAX = 3.4028234663852886e38
 
@@ -73,11 +74,13 @@ def tile_linearrtus_kernel(
         x_codes = keep.tile([P, CHUNKS, PASSES * CHUNK], U32, align_bytes=64)
         x_planes = keep.tile([P, CHUNKS, PASSES * CHUNK], U8, align_bytes=64)
         param_rows = keep.tile([P, P], BF16)
+        idle_work = keep.tile([P, 4 * P], BF16)
         ident_bf16 = keep.tile([P, P], BF16)
         ident_f32 = keep.tile([P, P], F32)
 
         nc.vector.memset(w_planes[:].bitcast(I32), 0)
         nc.vector.memset(param_rows[:], 0.0)
+        nc.vector.memset(idle_work[:], 0.0)
         make_identity(nc, ident_bf16[:])
         make_identity(nc, ident_f32[:])
 
@@ -126,6 +129,13 @@ def tile_linearrtus_kernel(
         load_weights(3)
         for c in range(1, CHUNKS):
             load_h(c, 0)
+
+        def keep_warm(count):
+            sink = psum_acc.tile([P, 4 * P], F32, tag="acc")
+            for unused in range(count):
+                nc.tensor.matmul(sink[:], lhsT=idle_work[:, 0:P], rhs=idle_work[:], start=True, stop=True)
+
+        keep_warm(WARM_FIRST)
 
         one = keep.tile([P, 1], F32)
         warm = keep.tile([P, 1], F32)
@@ -316,6 +326,7 @@ def tile_linearrtus_kernel(
             for g in range(PASSES):
                 transpose_x(c, g)
                 copy_x(c, g)
+                keep_warm(1)
             if c >= 1:
                 quantise_x(c - 1)
         quantise_x(CHUNKS - 1)

@@ -31,7 +31,6 @@ STORE_TILES = 4
 STORE_ROUNDS = STORE_TILES // ROUND_TILES
 LOAD_COLS = ROUND_TILES * P
 FIRST_H_PIECES = 2
-WARM_FIRST = 5
 TINY = 1e-30
 FLOAT32_MAX = 3.4028234663852886e38
 
@@ -74,13 +73,11 @@ def tile_linearrtus_kernel(
         x_codes = keep.tile([P, CHUNKS, PASSES * CHUNK], U32, align_bytes=64)
         x_planes = keep.tile([P, CHUNKS, PASSES * CHUNK], U8, align_bytes=64)
         param_rows = keep.tile([P, P], BF16)
-        idle_work = keep.tile([P, 4 * P], BF16)
         ident_bf16 = keep.tile([P, P], BF16)
         ident_f32 = keep.tile([P, P], F32)
 
         nc.vector.memset(w_planes[:].bitcast(I32), 0)
         nc.vector.memset(param_rows[:], 0.0)
-        nc.vector.memset(idle_work[:], 0.0)
         make_identity(nc, ident_bf16[:])
         make_identity(nc, ident_f32[:])
 
@@ -103,10 +100,6 @@ def tile_linearrtus_kernel(
         def load_x(c):
             nc.sync.dma_start(out=x_sb[:, c], in_=x_rows[:, c])
 
-        nc.sync.dma_start(out=param_rows[0:N_TILES, :], in_=r_param.rearrange("o (j n) -> (o j) n", n=P))
-        nc.sync.dma_start(
-            out=param_rows[N_TILES : 2 * N_TILES, :], in_=theta_param.rearrange("o (j n) -> (o j) n", n=P)
-        )
         def load_scales(w):
             for quadrant in range(4):
                 first = 32 * quadrant + 8 * w
@@ -116,26 +109,23 @@ def tile_linearrtus_kernel(
                 )
 
         load_x(0)
+        nc.sync.dma_start(out=param_rows[0:N_TILES, :], in_=r_param.rearrange("o (j n) -> (o j) n", n=P))
+        nc.sync.dma_start(
+            out=param_rows[N_TILES : 2 * N_TILES, :], in_=theta_param.rearrange("o (j n) -> (o j) n", n=P)
+        )
         load_x(1)
         load_scales(0)
         load_x(2)
-        load_x(3)
         load_scales(1)
         load_weights(0)
         load_h(0, 0)
         load_weights(1)
+        load_x(3)
         load_weights(2)
         load_h(0, 1)
         load_weights(3)
         for c in range(1, CHUNKS):
             load_h(c, 0)
-
-        def keep_warm(count):
-            sink = psum_acc.tile([P, 4 * P], F32, tag="acc")
-            for unused in range(count):
-                nc.tensor.matmul(sink[:], lhsT=idle_work[:, 0:P], rhs=idle_work[:], start=True, stop=True)
-
-        keep_warm(WARM_FIRST)
 
         one = keep.tile([P, 1], F32)
         warm = keep.tile([P, 1], F32)
@@ -144,7 +134,7 @@ def tile_linearrtus_kernel(
         param_ps = psum_back.tile([P, P], BF16, tag="back")
         nc.tensor.transpose(param_ps[:], param_rows[:], ident_bf16[:])
         params = keep.tile([P, 2 * N_TILES], F32)
-        nc.vector.tensor_copy(out=params[:], in_=param_ps[:, 0 : 2 * N_TILES])
+        nc.scalar.copy(out=params[:], in_=param_ps[:, 0 : 2 * N_TILES])
         radius = params[:, 0:N_TILES]
         theta = params[:, N_TILES : 2 * N_TILES]
 
@@ -159,32 +149,24 @@ def tile_linearrtus_kernel(
         is_open = keep.tile([P, N_TILES], F32)
         root = keep.tile([P, N_TILES], F32)
         norm = keep.tile([P, N_TILES], F32)
-        nc.vector.tensor_tensor(out=room[:], in0=radius, in1=radius, op=ALU.mult)
-        nc.vector.tensor_scalar(out=room[:], in0=room[:], scalar1=-1.0, scalar2=1.0, op0=ALU.mult, op1=ALU.add)
-        nc.vector.tensor_single_scalar(out=is_open[:], in_=room[:], scalar=0.0, op=ALU.is_gt)
-        nc.vector.tensor_scalar_max(out=room[:], in0=room[:], scalar1=TINY)
+        turn = keep.tile([P, N_TILES], F32)
+        nc.gpsimd.tensor_tensor(out=room[:], in0=radius, in1=radius, op=ALU.mult)
+        nc.gpsimd.tensor_scalar(out=room[:], in0=room[:], scalar1=-1.0, scalar2=1.0, op0=ALU.mult, op1=ALU.add)
+        nc.gpsimd.tensor_single_scalar(out=is_open[:], in_=room[:], scalar=0.0, op=ALU.is_gt)
+        nc.gpsimd.tensor_scalar_max(out=room[:], in0=room[:], scalar1=TINY)
         nc.scalar.activation(out=root[:], in_=room[:], func=ACT.Sqrt)
         nc.scalar.activation(out=sin_half[:], in_=theta, func=ACT.Sin, scale=0.5)
         nc.scalar.activation(out=sin_quarter[:], in_=theta, func=ACT.Sin, scale=0.25)
-
-        def finish_norm():
-            nc.vector.tensor_tensor(out=norm[:], in0=root[:], in1=is_open[:], op=ALU.mult)
-
-        def finish_rotation():
-            nc.vector.tensor_tensor(out=cos_full[:], in0=sin_half[:], in1=sin_half[:], op=ALU.mult)
-            nc.vector.tensor_scalar(
-                out=cos_full[:], in0=cos_full[:], scalar1=-2.0, scalar2=1.0, op0=ALU.mult, op1=ALU.add
-            )
-            nc.vector.tensor_tensor(out=gain[:], in0=cos_full[:], in1=radius, op=ALU.mult)
-            nc.vector.tensor_tensor(out=cos_half[:], in0=sin_quarter[:], in1=sin_quarter[:], op=ALU.mult)
-            nc.vector.tensor_scalar(
-                out=cos_half[:], in0=cos_half[:], scalar1=-2.0, scalar2=1.0, op0=ALU.mult, op1=ALU.add
-            )
-            nc.vector.tensor_tensor(out=phi[:], in0=sin_half[:], in1=cos_half[:], op=ALU.mult)
-            nc.vector.scalar_tensor_tensor(
-                out=phi[:], in0=phi[:], scalar=2.0, in1=radius, op0=ALU.mult, op1=ALU.mult
-            )
-            nc.vector.tensor_scalar_mul(out=neg_phi[:], in0=phi[:], scalar1=-1.0)
+        nc.gpsimd.tensor_tensor(out=norm[:], in0=root[:], in1=is_open[:], op=ALU.mult)
+        nc.gpsimd.tensor_tensor(out=cos_full[:], in0=sin_half[:], in1=sin_half[:], op=ALU.mult)
+        nc.gpsimd.tensor_scalar(out=cos_full[:], in0=cos_full[:], scalar1=-2.0, scalar2=1.0, op0=ALU.mult, op1=ALU.add)
+        nc.gpsimd.tensor_tensor(out=gain[:], in0=cos_full[:], in1=radius, op=ALU.mult)
+        nc.gpsimd.tensor_tensor(out=cos_half[:], in0=sin_quarter[:], in1=sin_quarter[:], op=ALU.mult)
+        nc.gpsimd.tensor_scalar(out=cos_half[:], in0=cos_half[:], scalar1=-2.0, scalar2=1.0, op0=ALU.mult, op1=ALU.add)
+        nc.gpsimd.tensor_tensor(out=turn[:], in0=sin_half[:], in1=cos_half[:], op=ALU.mult)
+        nc.gpsimd.tensor_tensor(out=turn[:], in0=turn[:], in1=radius, op=ALU.mult)
+        nc.gpsimd.tensor_scalar_mul(out=phi[:], in0=turn[:], scalar1=2.0)
+        nc.gpsimd.tensor_scalar_mul(out=neg_phi[:], in0=turn[:], scalar1=-2.0)
 
         xt_of = {}
 
@@ -202,7 +184,7 @@ def tile_linearrtus_kernel(
         def copy_x(c, g):
             xt = xt_of[(c, g)]
             pairs = x_grouped[:, c, :].bitcast(F32).rearrange("q (g b u) -> q g b u", g=PASSES, u=2)
-            if g == 0:
+            if c == 0 or (g == 0 and c < CHUNKS - 1):
                 nc.vector.tensor_copy(out=pairs[:, g], in_=xt[:].rearrange("q u b -> q b u"))
             else:
                 nc.scalar.copy(out=pairs[:, g], in_=xt[:].rearrange("q u b -> q b u"))
@@ -322,16 +304,13 @@ def tile_linearrtus_kernel(
                 for w in range(SIDES):
                     nc.sync.dma_start(out=relu_rows[:, c, :, w, n_cols], in_=relu[:, w])
 
-        for c in range(CHUNKS):
+        for c in range(CHUNKS - 1):
             for g in range(PASSES):
                 transpose_x(c, g)
                 copy_x(c, g)
-                keep_warm(1)
             if c >= 1:
                 quantise_x(c - 1)
-        quantise_x(CHUNKS - 1)
-        finish_norm()
-        finish_rotation()
+        quantise_x(CHUNKS - 2)
         multiply(0)
         scale(0)
         transpose_h(0)
@@ -343,7 +322,13 @@ def tile_linearrtus_kernel(
                 transpose_back(i - 1)
             if i + 1 < ROUNDS:
                 transpose_h(i + 1)
+            if i == 0:
+                for g in range(PASSES):
+                    transpose_x(CHUNKS - 1, g)
+                    copy_x(CHUNKS - 1, g)
             if i < ROUNDS:
                 rotate(i)
+            if i == 1:
+                quantise_x(CHUNKS - 1)
             if i >= 1:
                 relu_and_store(i - 1)

@@ -134,7 +134,7 @@ def tile_linearrtus_kernel(
         param_ps = psum_back.tile([P, P], BF16, tag="back")
         nc.tensor.transpose(param_ps[:], param_rows[:], ident_bf16[:])
         params = keep.tile([P, 2 * N_TILES], F32)
-        nc.scalar.copy(out=params[:], in_=param_ps[:, 0 : 2 * N_TILES])
+        nc.vector.tensor_copy(out=params[:], in_=param_ps[:, 0 : 2 * N_TILES])
         radius = params[:, 0:N_TILES]
         theta = params[:, N_TILES : 2 * N_TILES]
 
@@ -149,24 +149,32 @@ def tile_linearrtus_kernel(
         is_open = keep.tile([P, N_TILES], F32)
         root = keep.tile([P, N_TILES], F32)
         norm = keep.tile([P, N_TILES], F32)
-        turn = keep.tile([P, N_TILES], F32)
-        nc.gpsimd.tensor_tensor(out=room[:], in0=radius, in1=radius, op=ALU.mult)
-        nc.gpsimd.tensor_scalar(out=room[:], in0=room[:], scalar1=-1.0, scalar2=1.0, op0=ALU.mult, op1=ALU.add)
-        nc.gpsimd.tensor_single_scalar(out=is_open[:], in_=room[:], scalar=0.0, op=ALU.is_gt)
-        nc.gpsimd.tensor_scalar_max(out=room[:], in0=room[:], scalar1=TINY)
+        nc.vector.tensor_tensor(out=room[:], in0=radius, in1=radius, op=ALU.mult)
+        nc.vector.tensor_scalar(out=room[:], in0=room[:], scalar1=-1.0, scalar2=1.0, op0=ALU.mult, op1=ALU.add)
+        nc.vector.tensor_single_scalar(out=is_open[:], in_=room[:], scalar=0.0, op=ALU.is_gt)
+        nc.vector.tensor_scalar_max(out=room[:], in0=room[:], scalar1=TINY)
         nc.scalar.activation(out=root[:], in_=room[:], func=ACT.Sqrt)
         nc.scalar.activation(out=sin_half[:], in_=theta, func=ACT.Sin, scale=0.5)
         nc.scalar.activation(out=sin_quarter[:], in_=theta, func=ACT.Sin, scale=0.25)
-        nc.gpsimd.tensor_tensor(out=norm[:], in0=root[:], in1=is_open[:], op=ALU.mult)
-        nc.gpsimd.tensor_tensor(out=cos_full[:], in0=sin_half[:], in1=sin_half[:], op=ALU.mult)
-        nc.gpsimd.tensor_scalar(out=cos_full[:], in0=cos_full[:], scalar1=-2.0, scalar2=1.0, op0=ALU.mult, op1=ALU.add)
-        nc.gpsimd.tensor_tensor(out=gain[:], in0=cos_full[:], in1=radius, op=ALU.mult)
-        nc.gpsimd.tensor_tensor(out=cos_half[:], in0=sin_quarter[:], in1=sin_quarter[:], op=ALU.mult)
-        nc.gpsimd.tensor_scalar(out=cos_half[:], in0=cos_half[:], scalar1=-2.0, scalar2=1.0, op0=ALU.mult, op1=ALU.add)
-        nc.gpsimd.tensor_tensor(out=turn[:], in0=sin_half[:], in1=cos_half[:], op=ALU.mult)
-        nc.gpsimd.tensor_tensor(out=turn[:], in0=turn[:], in1=radius, op=ALU.mult)
-        nc.gpsimd.tensor_scalar_mul(out=phi[:], in0=turn[:], scalar1=2.0)
-        nc.gpsimd.tensor_scalar_mul(out=neg_phi[:], in0=turn[:], scalar1=-2.0)
+
+        def finish_norm():
+            nc.vector.tensor_tensor(out=norm[:], in0=root[:], in1=is_open[:], op=ALU.mult)
+
+        def finish_rotation():
+            nc.vector.tensor_tensor(out=cos_full[:], in0=sin_half[:], in1=sin_half[:], op=ALU.mult)
+            nc.vector.tensor_scalar(
+                out=cos_full[:], in0=cos_full[:], scalar1=-2.0, scalar2=1.0, op0=ALU.mult, op1=ALU.add
+            )
+            nc.vector.tensor_tensor(out=gain[:], in0=cos_full[:], in1=radius, op=ALU.mult)
+            nc.vector.tensor_tensor(out=cos_half[:], in0=sin_quarter[:], in1=sin_quarter[:], op=ALU.mult)
+            nc.vector.tensor_scalar(
+                out=cos_half[:], in0=cos_half[:], scalar1=-2.0, scalar2=1.0, op0=ALU.mult, op1=ALU.add
+            )
+            nc.vector.tensor_tensor(out=phi[:], in0=sin_half[:], in1=cos_half[:], op=ALU.mult)
+            nc.vector.scalar_tensor_tensor(
+                out=phi[:], in0=phi[:], scalar=2.0, in1=radius, op0=ALU.mult, op1=ALU.mult
+            )
+            nc.vector.tensor_scalar_mul(out=neg_phi[:], in0=phi[:], scalar1=-1.0)
 
         xt_of = {}
 
@@ -310,6 +318,9 @@ def tile_linearrtus_kernel(
                 copy_x(c, g)
             if c >= 1:
                 quantise_x(c - 1)
+            if c == 1:
+                finish_norm()
+                finish_rotation()
         quantise_x(CHUNKS - 2)
         multiply(0)
         scale(0)

@@ -29,7 +29,7 @@ ROUNDS_PER_CHUNK = N_TILES // ROUND_TILES
 ROUNDS = CHUNKS * ROUNDS_PER_CHUNK
 STORE_TILES = 4
 STORE_ROUNDS = STORE_TILES // ROUND_TILES
-LOAD_COLS = ROUND_TILES * P
+WEIGHT_TILES = (2, 2, 2, 2)
 FIRST_H_PIECES = 2
 TINY = 1e-30
 FLOAT32_MAX = 3.4028234663852886e38
@@ -58,16 +58,25 @@ def tile_linearrtus_kernel(
 
         x_sb = keep.tile([P, CHUNKS, SUB, D], BF16)
         h_sb = {}
+        h_tail = []
         for side in range(SIDES):
-            for c in range(CHUNKS):
+            for c in range(CHUNKS - 2):
                 pieces = FIRST_H_PIECES if c == 0 else 1
                 h_sb[(side, c)] = [
                     keep.tile([P, SUB, H // pieces], BF16, name="h%d_%d_%d" % (side, c, piece))
                     for piece in range(pieces)
                 ]
-        w1_codes = keep.tile([P, PASSES, H], U32, align_bytes=64)
-        w2_codes = keep.tile([P, PASSES, H], U32, align_bytes=64)
-        w_codes = (w1_codes, w2_codes)
+            tail = keep.tile([P, 2, SUB, H], BF16, name="h%d_tail" % side)
+            h_tail.append(tail)
+            for k in range(2):
+                h_sb[(side, CHUNKS - 2 + k)] = [tail[:, k]]
+        w_codes = [
+            [
+                keep.tile([P, PASSES, tiles * P], U32, align_bytes=64, name="w%d_codes_%d" % (w, piece))
+                for piece, tiles in enumerate(WEIGHT_TILES)
+            ]
+            for w in range(SIDES)
+        ]
         w_planes = keep.tile([P, H], U8, align_bytes=64)
         x_grouped = keep.tile([P, CHUNKS, PASSES * CHUNK * PACK], BF16, align_bytes=64)
         x_codes = keep.tile([P, CHUNKS, PASSES * CHUNK], U32, align_bytes=64)
@@ -82,11 +91,11 @@ def tile_linearrtus_kernel(
         make_identity(nc, ident_f32[:])
 
         def load_weights(piece):
-            cols = slice(piece * LOAD_COLS, (piece + 1) * LOAD_COLS)
-            byte_cols = slice(piece * LOAD_COLS * PACK, (piece + 1) * LOAD_COLS * PACK)
+            first = sum(WEIGHT_TILES[:piece]) * P
+            byte_cols = slice(first * PACK, (first + WEIGHT_TILES[piece] * P) * PACK)
             for w in range(SIDES):
                 nc.sync.dma_start(
-                    out=w_codes[w][:, :, cols].bitcast(I32),
+                    out=w_codes[w][piece][:].bitcast(I32),
                     in_=words_dram[w].rearrange("g p n t -> p g (n t)")[:, :, byte_cols].bitcast(I32),
                 )
 
@@ -95,6 +104,13 @@ def tile_linearrtus_kernel(
                 width = H // len(h_sb[(side, c)])
                 nc.sync.dma_start(
                     out=h_sb[(side, c)][piece][:], in_=h_rows[side][:, c, :, piece * width : (piece + 1) * width]
+                )
+
+        def load_h_tail():
+            for side in range(SIDES):
+                nc.sync.dma_start(
+                    out=h_tail[side][:].rearrange("p c s n -> p (c s n)"),
+                    in_=h_rows[side][:, CHUNKS - 2 :].rearrange("p c s n -> p (c s n)"),
                 )
 
         def load_x(c):
@@ -124,8 +140,8 @@ def tile_linearrtus_kernel(
         load_weights(2)
         load_h(0, 1)
         load_weights(3)
-        for c in range(1, CHUNKS):
-            load_h(c, 0)
+        load_h(1, 0)
+        load_h_tail()
 
         one = keep.tile([P, 1], F32)
         warm = keep.tile([P, 1], F32)
@@ -228,6 +244,13 @@ def tile_linearrtus_kernel(
                         )
             ht_of[i] = ht
 
+        def code_tile(w, g, j):
+            piece, local = 0, j
+            while local >= WEIGHT_TILES[piece]:
+                local -= WEIGHT_TILES[piece]
+                piece += 1
+            return w_codes[w][piece][:, g, local * P : (local + 1) * P]
+
         def multiply(i):
             c, first_tile = place(i)
             for t in range(ROUND_TILES):
@@ -238,7 +261,7 @@ def tile_linearrtus_kernel(
                         b_cols = slice(g * CHUNK, (g + 1) * CHUNK)
                         nc.tensor.matmul_mx(
                             out=acc[:, w, :],
-                            lhsT=w_codes[w][:, g, n_cols].bitcast(FP8X4),
+                            lhsT=code_tile(w, g, first_tile + t).bitcast(FP8X4),
                             lhsT_scale=w_planes[8 * w + 4 * g : P, n_cols],
                             rhs=x_codes[:, c, b_cols].bitcast(FP8X4),
                             rhs_scale=x_planes[:, c, b_cols],

from contextlib import ExitStack

import concourse.mybir as mybir
from concourse.masks import make_identity

FP8X4 = mybir.dt.float8_e4m3fn_x4
BF16 = mybir.dt.bfloat16
F32 = mybir.dt.float32
I32 = mybir.dt.int32
U32 = mybir.dt.uint32
U8 = mybir.dt.uint8
ALU = mybir.AluOpType
ACT = mybir.ActivationFunctionType

B, D, H = 1024, 1024, 1024
FLOPS = 2 * B * D * 2 * H

P = 128
PACK = 4
K_PASS = P * PACK
PASSES = D // K_PASS
SUB = 2
CHUNK = SUB * P
CHUNKS = B // CHUNK
N_TILES = H // P
SIDES = 2
ROUND_TILES = 2
ROUNDS_PER_CHUNK = N_TILES // ROUND_TILES
ROUNDS = CHUNKS * ROUNDS_PER_CHUNK
STORE_TILES = 4
STORE_ROUNDS = STORE_TILES // ROUND_TILES
WEIGHT_TILES = (2, 2, 2, 2)
FIRST_H_PIECES = 2
TINY = 1e-30
FLOAT32_MAX = 3.4028234663852886e38


def tile_linearrtus_kernel(
    tc, h_c1, h_c2, x_t, r_param, theta_param, w1_words, w1_scales, w2_words, w2_scales, out_0, out_1, out_2
):
    nc = tc.nc
    with ExitStack() as ctx:
        keep = ctx.enter_context(tc.tile_pool(name="keep", bufs=1))
        work = ctx.enter_context(tc.tile_pool(name="work", bufs=3 * ROUND_TILES))
        outs = ctx.enter_context(tc.tile_pool(name="outs", bufs=4))
        psum_acc = ctx.enter_context(tc.psum_pool(name="psum_acc", bufs=3))
        psum_ht = ctx.enter_context(tc.psum_pool(name="psum_ht", bufs=2))
        psum_back = ctx.enter_context(tc.psum_pool(name="psum_back", bufs=3))
        ctx.enter_context(tc.manual_schedule())

        by_chunk = "(p c s) n -> p c s n"
        x_rows = x_t.rearrange(by_chunk, c=CHUNKS, s=SUB)
        h_rows = [h.rearrange(by_chunk, c=CHUNKS, s=SUB) for h in (h_c1, h_c2)]
        state_rows = [o.rearrange(by_chunk, c=CHUNKS, s=SUB) for o in (out_0, out_1)]
        relu_rows = out_2.rearrange("(p c s) (w n) -> p c s w n", c=CHUNKS, s=SUB, w=SIDES)
        words_dram = (w1_words, w2_words)
        scales_dram = (w1_scales, w2_scales)

        x_sb = keep.tile([P, CHUNKS, SUB, D], BF16)
        h_sb = {}
        h_tail = []
        for side in range(SIDES):
            for c in range(CHUNKS - 2):
                pieces = FIRST_H_PIECES if c == 0 else 1
                h_sb[(side, c)] = [
                    keep.tile([P, SUB, H // pieces], BF16, name="h%d_%d_%d" % (side, c, piece))
                    for piece in range(pieces)
                ]
            tail = keep.tile([P, 2, SUB, H], BF16, name="h%d_tail" % side)
            h_tail.append(tail)
            for k in range(2):
                h_sb[(side, CHUNKS - 2 + k)] = [tail[:, k]]
        w_codes = [
            [
                keep.tile([P, PASSES, tiles * P], U32, align_bytes=64, name="w%d_codes_%d" % (w, piece))
                for piece, tiles in enumerate(WEIGHT_TILES)
            ]
            for w in range(SIDES)
        ]
        w_planes = keep.tile([P, H], U8, align_bytes=64)
        x_grouped = keep.tile([P, CHUNKS, PASSES * CHUNK * PACK], BF16, align_bytes=64)
        x_codes = keep.tile([P, CHUNKS, PASSES * CHUNK], U32, align_bytes=64)
        x_planes = keep.tile([P, CHUNKS, PASSES * CHUNK], U8, align_bytes=64)
        param_rows = keep.tile([P, P], BF16)
        ident_bf16 = keep.tile([P, P], BF16)
        ident_f32 = keep.tile([P, P], F32)

        nc.vector.memset(w_planes[:].bitcast(I32), 0)
        nc.vector.memset(param_rows[:], 0.0)
        make_identity(nc, ident_bf16[:])
        make_identity(nc, ident_f32[:])

        def load_weights(piece):
            first = sum(WEIGHT_TILES[:piece]) * P
            byte_cols = slice(first * PACK, (first + WEIGHT_TILES[piece] * P) * PACK)
            for w in range(SIDES):
                nc.sync.dma_start(
                    out=w_codes[w][piece][:].bitcast(I32),
                    in_=words_dram[w].rearrange("g p n t -> p g (n t)")[:, :, byte_cols].bitcast(I32),
                )

        def load_h(c, piece):
            for side in range(SIDES):
                width = H // len(h_sb[(side, c)])
                nc.sync.dma_start(
                    out=h_sb[(side, c)][piece][:], in_=h_rows[side][:, c, :, piece * width : (piece + 1) * width]
                )

        def load_h_tail():
            for side in range(SIDES):
                nc.sync.dma_start(
                    out=h_tail[side][:].rearrange("p c s n -> p (c s n)"),
                    in_=h_rows[side][:, CHUNKS - 2 :].rearrange("p c s n -> p (c s n)"),
                )

        def load_x(c):
            nc.sync.dma_start(out=x_sb[:, c], in_=x_rows[:, c])

        def load_scales(w):
            for quadrant in range(4):
                first = 32 * quadrant + 8 * w
                nc.sync.dma_start(
                    out=w_planes[first : first + 8, :].bitcast(I32),
                    in_=scales_dram[w][:, 4 * quadrant : 4 * quadrant + 4, :].bitcast(I32),
                )

        load_x(0)
        nc.sync.dma_start(out=param_rows[0:N_TILES, :], in_=r_param.rearrange("o (j n) -> (o j) n", n=P))
        nc.sync.dma_start(
            out=param_rows[N_TILES : 2 * N_TILES, :], in_=theta_param.rearrange("o (j n) -> (o j) n", n=P)
        )
        load_x(1)
        load_scales(0)
        load_x(2)
        load_scales(1)
        load_weights(0)
        load_h(0, 0)
        load_weights(1)
        load_x(3)
        load_weights(2)
        load_h(0, 1)
        load_weights(3)
        load_h(1, 0)
        load_h_tail()

        one = keep.tile([P, 1], F32)
        warm = keep.tile([P, 1], F32)
        nc.vector.memset(one[:], 1.0)
        nc.scalar.activation(out=warm[:], in_=one[:], func=ACT.Sqrt)
        param_ps = psum_back.tile([P, P], BF16, tag="back")
        nc.tensor.transpose(param_ps[:], param_rows[:], ident_bf16[:])
        params = keep.tile([P, 2 * N_TILES], F32)
        nc.vector.tensor_copy(out=params[:], in_=param_ps[:, 0 : 2 * N_TILES])
        radius = params[:, 0:N_TILES]
        theta = params[:, N_TILES : 2 * N_TILES]

        sin_half = keep.tile([P, N_TILES], F32)
        sin_quarter = keep.tile([P, N_TILES], F32)
        cos_half = keep.tile([P, N_TILES], F32)
        cos_full = keep.tile([P, N_TILES], F32)
        gain = keep.tile([P, N_TILES], F32)
        phi = keep.tile([P, N_TILES], F32)
        neg_phi = keep.tile([P, N_TILES], F32)
        room = keep.tile([P, N_TILES], F32)
        is_open = keep.tile([P, N_TILES], F32)
        root = keep.tile([P, N_TILES], F32)
        norm = keep.tile([P, N_TILES], F32)
        nc.vector.tensor_tensor(out=room[:], in0=radius, in1=radius, op=ALU.mult)
        nc.vector.tensor_scalar(out=room[:], in0=room[:], scalar1=-1.0, scalar2=1.0, op0=ALU.mult, op1=ALU.add)
        nc.vector.tensor_single_scalar(out=is_open[:], in_=room[:], scalar=0.0, op=ALU.is_gt)
        nc.vector.tensor_scalar_max(out=room[:], in0=room[:], scalar1=TINY)
        nc.scalar.activation(out=root[:], in_=room[:], func=ACT.Sqrt)
        nc.scalar.activation(out=sin_half[:], in_=theta, func=ACT.Sin, scale=0.5)
        nc.scalar.activation(out=sin_quarter[:], in_=theta, func=ACT.Sin, scale=0.25)

        def finish_norm():
            nc.vector.tensor_tensor(out=norm[:], in0=root[:], in1=is_open[:], op=ALU.mult)

        def finish_rotation():
            nc.vector.tensor_tensor(out=cos_full[:], in0=sin_half[:], in1=sin_half[:], op=ALU.mult)
            nc.vector.tensor_scalar(
                out=cos_full[:], in0=cos_full[:], scalar1=-2.0, scalar2=1.0, op0=ALU.mult, op1=ALU.add
            )
            nc.vector.tensor_tensor(out=gain[:], in0=cos_full[:], in1=radius, op=ALU.mult)
            nc.vector.tensor_tensor(out=cos_half[:], in0=sin_quarter[:], in1=sin_quarter[:], op=ALU.mult)
            nc.vector.tensor_scalar(
                out=cos_half[:], in0=cos_half[:], scalar1=-2.0, scalar2=1.0, op0=ALU.mult, op1=ALU.add
            )
            nc.vector.tensor_tensor(out=phi[:], in0=sin_half[:], in1=cos_half[:], op=ALU.mult)
            nc.vector.scalar_tensor_tensor(
                out=phi[:], in0=phi[:], scalar=2.0, in1=radius, op0=ALU.mult, op1=ALU.mult
            )
            nc.vector.tensor_scalar_mul(out=neg_phi[:], in0=phi[:], scalar1=-1.0)

        xt_of = {}

        def transpose_x(c, g):
            xt = psum_back.tile([P, 2, CHUNK], F32, tag="back")
            for u in range(2):
                for s in range(SUB):
                    words = x_sb[:, c, s, :].bitcast(F32)
                    first = g * (K_PASS // 2) + u
                    nc.tensor.transpose(
                        xt[:, u, s * P : (s + 1) * P], words[:, first : (g + 1) * (K_PASS // 2) : 2], ident_f32[:]
                    )
            xt_of[(c, g)] = xt

        def copy_x(c, g):
            xt = xt_of[(c, g)]
            pairs = x_grouped[:, c, :].bitcast(F32).rearrange("q (g b u) -> q g b u", g=PASSES, u=2)
            if c == 0 or (g == 0 and c < CHUNKS - 1):
                nc.vector.tensor_copy(out=pairs[:, g], in_=xt[:].rearrange("q u b -> q b u"))
            else:
                nc.scalar.copy(out=pairs[:, g], in_=xt[:].rearrange("q u b -> q b u"))

        def quantise_x(c):
            nc.vector.quantize_mx(
                out=x_codes[:, c, :].bitcast(FP8X4), scales=x_planes[:, c, :], in_=x_grouped[:, c, :]
            )

        ht_of = {}
        acc_of = {}
        scaled_of = {}
        state_of = {}
        out_of = {}

        def place(i):
            return i // ROUNDS_PER_CHUNK, (i % ROUNDS_PER_CHUNK) * ROUND_TILES

        def h_block(side, c, s, j):
            pieces = h_sb[(side, c)]
            tiles_per_piece = N_TILES // len(pieces)
            local = j % tiles_per_piece
            return pieces[j // tiles_per_piece][:, s, local * P : (local + 1) * P]

        def transpose_h(i):
            c, first_tile = place(i)
            ht = psum_ht.tile([P, ROUND_TILES, SIDES, CHUNK], BF16)
            for t in range(ROUND_TILES):
                for side in range(SIDES):
                    for s in range(SUB):
                        nc.tensor.transpose(
                            ht[:, t, side, s * P : (s + 1) * P], h_block(side, c, s, first_tile + t), ident_bf16[:]
                        )
            ht_of[i] = ht

        def code_tile(w, g, j):
            piece, local = 0, j
            while local >= WEIGHT_TILES[piece]:
                local -= WEIGHT_TILES[piece]
                piece += 1
            return w_codes[w][piece][:, g, local * P : (local + 1) * P]

        def multiply(i):
            c, first_tile = place(i)
            for t in range(ROUND_TILES):
                n_cols = slice((first_tile + t) * P, (first_tile + t + 1) * P)
                acc = psum_acc.tile([P, SIDES, CHUNK], F32)
                for w in range(SIDES):
                    for g in range(PASSES):
                        b_cols = slice(g * CHUNK, (g + 1) * CHUNK)
                        nc.tensor.matmul_mx(
                            out=acc[:, w, :],
                            lhsT=code_tile(w, g, first_tile + t).bitcast(FP8X4),
                            lhsT_scale=w_planes[8 * w + 4 * g : P, n_cols],
                            rhs=x_codes[:, c, b_cols].bitcast(FP8X4),
                            rhs_scale=x_planes[:, c, b_cols],
                            start=(g == 0),
                            stop=(g == PASSES - 1),
                        )
                acc_of[(i, t)] = acc

        def scale(i):
            first_tile = place(i)[1]
            for t in range(ROUND_TILES):
                j = first_tile + t
                scaled = work.tile([P, SIDES, CHUNK], F32)
                nc.scalar.activation(out=scaled[:], in_=acc_of[(i, t)][:], func=ACT.Copy, scale=norm[:, j : j + 1])
                scaled_of[(i, t)] = scaled

        def rotate(i):
            first_tile = place(i)[1]
            ht = ht_of[i]
            partial_of = {}
            for t in range(ROUND_TILES):
                j = first_tile + t
                partial = work.tile([P, SIDES, CHUNK], F32)
                nc.vector.scalar_tensor_tensor(
                    out=partial[:], in0=ht[:, t], scalar=gain[:, j : j + 1], in1=scaled_of[(i, t)][:],
                    op0=ALU.mult, op1=ALU.add,
                )
                partial_of[t] = partial
            for t in range(ROUND_TILES):
                j = first_tile + t
                state = work.tile([P, SIDES, CHUNK], F32)
                nc.vector.scalar_tensor_tensor(
                    out=state[:, 0], in0=ht[:, t, 1], scalar=neg_phi[:, j : j + 1], in1=partial_of[t][:, 0],
                    op0=ALU.mult, op1=ALU.add,
                )
                nc.vector.scalar_tensor_tensor(
                    out=state[:, 1], in0=ht[:, t, 0], scalar=phi[:, j : j + 1], in1=partial_of[t][:, 1],
                    op0=ALU.mult, op1=ALU.add,
                )
                state_of[(i, t)] = state

        def transpose_back(i):
            group_tile = place(i)[1] % STORE_TILES
            if group_tile == 0:
                plain = outs.tile([P, SIDES, SUB, STORE_TILES * P], F32)
                relu = outs.tile([P, SIDES, SUB, STORE_TILES * P], F32)
                out_of[i // STORE_ROUNDS] = (plain, relu)
            plain = out_of[i // STORE_ROUNDS][0]
            for t in range(ROUND_TILES):
                state = state_of[(i, t)]
                back = psum_back.tile([P, SIDES, SUB, P], F32)
                for w in range(SIDES):
                    for s in range(SUB):
                        nc.tensor.transpose(back[:, w, s, :], state[:, w, s * P : (s + 1) * P], ident_f32[:])
                cols = slice((group_tile + t) * P, (group_tile + t + 1) * P)
                nc.scalar.copy(out=plain[:, :, :, cols], in_=back[:])

        def relu_and_store(i):
            c, first_tile = place(i)
            group_tile = first_tile % STORE_TILES
            plain, relu = out_of[i // STORE_ROUNDS]
            cols = slice(group_tile * P, (group_tile + ROUND_TILES) * P)
            nc.gpsimd.tensor_scalar(
                out=relu[:, :, :, cols], in0=plain[:, :, :, cols], scalar1=FLOAT32_MAX, scalar2=0.0,
                op0=ALU.min, op1=ALU.max,
            )
            if group_tile + ROUND_TILES == STORE_TILES:
                n_cols = slice((first_tile + ROUND_TILES - STORE_TILES) * P, (first_tile + ROUND_TILES) * P)
                for w in range(SIDES):
                    nc.sync.dma_start(out=state_rows[w][:, c, :, n_cols], in_=plain[:, w])
                for w in range(SIDES):
                    nc.sync.dma_start(out=relu_rows[:, c, :, w, n_cols], in_=relu[:, w])

        for c in range(CHUNKS - 1):
            for g in range(PASSES):
                transpose_x(c, g)
                copy_x(c, g)
            if c >= 1:
                quantise_x(c - 1)
            if c == 1:
                finish_norm()
                finish_rotation()
        quantise_x(CHUNKS - 2)
        multiply(0)
        scale(0)
        transpose_h(0)
        for i in range(ROUNDS + 1):
            if i + 1 < ROUNDS:
                multiply(i + 1)
                scale(i + 1)
            if i >= 1:
                transpose_back(i - 1)
            if i + 1 < ROUNDS:
                transpose_h(i + 1)
            if i == 0:
                for g in range(PASSES):
                    transpose_x(CHUNKS - 1, g)
                    copy_x(CHUNKS - 1, g)
            if i < ROUNDS:
                rotate(i)
            if i == 1:
                quantise_x(CHUNKS - 1)
            if i >= 1:
                relu_and_store(i - 1)
